import numpy as np
import ml_dtypes


def mxq(x, axis, fmt="e4m3"):
    dtype, down = {"e4m3": (ml_dtypes.float8_e4m3fn, 7), "e5m2": (ml_dtypes.float8_e5m2, 14)}[fmt]
    v = np.moveaxis(np.asarray(x, np.float32).astype(ml_dtypes.bfloat16).astype(np.float64), axis, -1)
    blocks = v.reshape(v.shape[:-1] + (-1, 32))
    amax = np.abs(blocks).max(-1, keepdims=True)
    byte = np.maximum(np.where(amax > 0, np.frexp(amax)[1] - 1 + 127, 0) - down, 1)
    scale = np.exp2(byte - 127.0)
    codes = (blocks / scale).astype(np.float32).astype(dtype).astype(np.float64)
    return np.moveaxis((codes * scale).reshape(v.shape), -1, axis)


WIDE = False


def mx_kscale(k):
    if not WIDE:
        return np.ones(k)
    levels = np.array([10, -10, 5, -5, 0])
    a = np.random.permutation(np.resize(levels, k // 512 * 4)).reshape(k // 512, 4)
    idx = np.arange(k)
    return np.exp2(a[idx // 512, idx % 128 // 32])


BF16 = ml_dtypes.bfloat16


def bf(x):
    return np.asarray(x, np.float32).astype(BF16)


def f64(x):
    return np.asarray(x).astype(np.float64)


B, IN, H = 512, 1024, 1024
QH = H % (16 * 32) == 0


def sigmoid(v):
    return 1.0 / (1.0 + np.exp(-v))


def setup_inputs():
    s = mx_kscale(IN)
    one = np.ones(H)
    inp = {"x": bf(np.random.standard_normal((B, IN)) * s), "hidden": bf(np.random.standard_normal((B, H)))}
    for name, fan_in, f in (("Wir", IN, s), ("Whr", H, one), ("Wiz", IN, s), ("Whz", H, one), ("Win", IN, s), ("Whn", H, one)):
        inp[name + "_w"] = bf(np.random.standard_normal((H, fan_in)) / np.sqrt(fan_in) / f[None, :])
        inp[name + "_b"] = bf(np.random.standard_normal(H) * 0.2)
    return inp


def reference(x, hidden, Wir_w, Wir_b, Whr_w, Whr_b, Wiz_w, Wiz_b, Whz_w, Whz_b, Win_w, Win_b, Whn_w, Whn_b):
    x, hidden = f64(x), f64(hidden)
    Wi = np.concatenate([f64(Wir_w), f64(Wiz_w), f64(Win_w)], axis=0)
    Wh = np.concatenate([f64(Whr_w), f64(Whz_w), f64(Whn_w)], axis=0)
    bi = np.concatenate([f64(Wir_b), f64(Wiz_b), f64(Win_b)], axis=0)
    bh = np.concatenate([f64(Whr_b), f64(Whz_b), f64(Whn_b)], axis=0)
    gi = (mxq(x, 1, "e4m3") @ mxq(Wi, 1, "e4m3").T) + bi
    if QH:
        gh = (mxq(hidden, 1, "e4m3") @ mxq(Wh, 1, "e4m3").T) + bh
    else:
        gh = hidden @ Wh.T + bh
    ir, iz, inn = np.split(gi, 3, axis=1)
    hr, hz, hn = np.split(gh, 3, axis=1)
    rt = sigmoid(ir + hr)
    zt = sigmoid(iz + hz)
    nt = np.tanh(inn + rt * hn)
    ht = (1.0 - zt) * nt + zt * hidden
    return ht

@@ -1,0 +1,350 @@
+from contextlib import ExitStack
+
+import concourse.masks as masks
+import concourse.mybir as mybir
+
+F32 = mybir.dt.float32
+BF16 = mybir.dt.bfloat16
+U32 = mybir.dt.uint32
+U8 = mybir.dt.uint8
+FP8X4 = mybir.dt.float8_e4m3fn_x4
+ALU = mybir.AluOpType
+ACTF = mybir.ActivationFunctionType
+
+P = 128
+B = 512
+K = 1024
+H = 1024
+FLOPS = 2 * B * K * H * 6
+
+PINNED = True
+
+IR, HR, HN, IN, IZ, HZ = 0, 1, 2, 3, 4, 5
+SRC = ["x", "h", "h", "x", "x", "h"]
+GATE = ["r", "r", "hn", "in", "z", "z"]
+OPENS = [True, False, True, True, True, False]
+CLOSES = [False, True, True, True, False, True]
+ORDER0 = [IR, IN, HR, HN, IZ, HZ]
+ORDER = [IR, HR, HN, IN, IZ, HZ]
+
+
+def tile_gru_kernel(tc, x, hidden, Wir_w, Wir_b, Whr_w, Whr_b, Wiz_w, Wiz_b, Whz_w, Whz_b,
+                               Win_w, Win_b, Whn_w, Whn_b, out):
+    nc = tc.nc
+    weights = [Wir_w, Whr_w, Whn_w, Win_w, Wiz_w, Whz_w]
+    biases = [Wir_b, Whr_b, Wiz_b, Whz_b, Win_b, Whn_b]
+    units = [(w, 0) for w in ORDER0] + [(w, s) for s in range(1, 4) for w in ORDER]
+    with ExitStack() as ctx:
+        if PINNED:
+            ctx.enter_context(tc.manual_schedule())
+        const = ctx.enter_context(tc.tile_pool(name="const", bufs=1))
+        raw = ctx.enter_context(tc.tile_pool(name="raw", bufs=1))
+        keep = ctx.enter_context(tc.tile_pool(name="keep", bufs=1))
+        grp = ctx.enter_context(tc.tile_pool(name="grp", bufs=4))
+        cod = ctx.enter_context(tc.tile_pool(name="cod", bufs=6))
+        ep = ctx.enter_context(tc.tile_pool(name="ep", bufs=4))
+        osb = ctx.enter_context(tc.tile_pool(name="osb", bufs=2))
+        pt = ctx.enter_context(tc.psum_pool(name="pt", bufs=4))
+        pg = ctx.enter_context(tc.psum_pool(name="pg", bufs=4))
+
+        b_raw = const.tile([P, 2 * P], BF16, name="b_raw")
+        nc.vector.memset(b_raw[:], 0.0)
+        for v in range(6):
+            nc.scalar.dma_start(out=b_raw[4 * v:4 * v + 4, :], in_=biases[v].rearrange("(s c) -> s c", s=4))
+        ident = const.tile([P, P], F32, name="ident")
+        masks.make_identity(nc, ident[:])
+        warm = const.tile([P, 1], F32, name="warm")
+        nc.vector.memset(warm[:], 0.0)
+        nc.scalar.activation(out=warm[:], in_=warm[:], func=ACTF.Sigmoid)
+
+        act_raw = {}
+        for nm in ("x", "h"):
+            act_raw[nm] = raw.tile([P, 4 * K], BF16, name="raw_" + nm)
+        w_raw = []
+        for n in range(24):
+            w_raw.append(raw.tile([P, 2 * K], BF16, name="w_raw_%d" % n))
+
+        def load_act(nm, src):
+            view = src.rearrange("(q j) k -> q (j k)", j=4)
+            for half in range(2):
+                cols = slice(half * 2 * K, (half + 1) * 2 * K)
+                nc.sync.dma_start(out=act_raw[nm][:, cols], in_=view[:, cols])
+
+        def load_w(n):
+            w, s = units[n]
+            view = weights[w].rearrange("(s q e) k -> s q (e k)", s=4, e=2)
+            nc.sync.dma_start(out=w_raw[n][:], in_=view[s])
+
+        load_act("x", x)
+        load_w(0)
+        load_w(1)
+        load_act("h", hidden)
+        for n in range(2, 24):
+            load_w(n)
+
+        banks = {}
+
+        def transposes(key, words):
+            bank = pt.tile([P, 4, P], F32, name="tb", tag="tb")
+            for c in range(4):
+                nc.tensor.transpose(bank[:, c, :], words[:, c * P:(c + 1) * P], ident[:])
+            banks[key] = bank
+
+        def copy_out(eng, dst, src):
+            if eng == "s":
+                nc.scalar.copy(out=dst, in_=src)
+            else:
+                nc.vector.tensor_copy(out=dst, in_=src)
+
+        a_grp, a_cod, a_scl = {}, {}, {}
+        for nm in ("x", "h"):
+            a_grp[nm] = keep.tile([P, 4 * K], BF16, name="grp_" + nm, align_bytes=64)
+            a_cod[nm] = keep.tile([P, K], U32, name="cod_" + nm, align_bytes=64)
+            a_scl[nm] = keep.tile([P, K], U8, name="scl_" + nm, align_bytes=64)
+
+        def AT(nm, j):
+            transposes((nm, j), act_raw[nm][:].bitcast(F32)[:, j * 512:(j + 1) * 512])
+
+        def AE(nm, j, eng):
+            dst = a_grp[nm][:].bitcast(F32)[:, j * 512:(j + 1) * 512].rearrange("p (g q u) -> p g q u", g=2, u=2)
+            copy_out(eng, dst, banks[(nm, j)].rearrange("p (g u) q -> p g q u", g=2))
+
+        def AQ(nm, j):
+            for g in range(2):
+                cols = slice(g * B + j * P, g * B + (j + 1) * P)
+                nc.vector.quantize_mx(out=a_cod[nm][:, cols].bitcast(FP8X4), scales=a_scl[nm][:, cols],
+                                      in_=a_grp[nm][:, (2 * j + g) * 512:(2 * j + g + 1) * 512])
+
+        bias_f = const.tile([P, 64], F32, name="bias_f")
+        bias_s = const.tile([P, 16], F32, name="bias_s")
+
+        def BIAS():
+            bank = pt.tile([P, 4, P], F32, name="tb", tag="tb")
+            nc.tensor.transpose(bank[:, 0, :], b_raw[:].bitcast(F32), ident[:])
+            bias_w = const.tile([P, 32], F32, name="bias_w")
+            nc.vector.tensor_copy(out=bias_w[:], in_=bank[:, 0, 0:32])
+            nc.vector.tensor_copy(out=bias_f[:], in_=bias_w[:].bitcast(BF16))
+            nc.vector.tensor_tensor(out=bias_s[:, 0:8], in0=bias_f[:, 0:8], in1=bias_f[:, 8:16], op=ALU.add)
+            nc.vector.tensor_tensor(out=bias_s[:, 8:16], in0=bias_f[:, 16:24], in1=bias_f[:, 24:32], op=ALU.add)
+
+        w_grp, w_cod, w_scl = {}, {}, {}
+
+        def TR(n, e):
+            transposes((n, e), w_raw[n][:].bitcast(F32)[:, e * 512:(e + 1) * 512])
+
+        def EV(n, e, eng="s"):
+            if n not in w_grp:
+                w_grp[n] = grp.tile([P, 2 * K], BF16, name="w_grp", tag="w_grp", align_bytes=64)
+            dst = w_grp[n][:].bitcast(F32)[:, e * 512:(e + 1) * 512].rearrange("p (g q u) -> p g q u", g=2, u=2)
+            copy_out(eng, dst, banks[(n, e)].rearrange("p (g u) q -> p g q u", g=2))
+
+        def QU(n):
+            w_cod[n] = cod.tile([P, 512], U32, name="w_cod", tag="w_cod", align_bytes=64)
+            w_scl[n] = cod.tile([P, 512], U8, name="w_scl", tag="w_scl", align_bytes=64)
+            nc.vector.quantize_mx(out=w_cod[n][:].bitcast(FP8X4), scales=w_scl[n][:], in_=w_grp[n][:])
+
+        acc = {}
+
+        def mx_pass(bank, n, e, g, c0, c1, start, stop):
+            nm = SRC[units[n][0]]
+            wc = slice(e * 256 + g * P, e * 256 + (g + 1) * P)
+            ac = slice(g * B + c0, g * B + c1)
+            nc.tensor.matmul_mx(out=bank, lhsT=w_cod[n][:, wc].bitcast(FP8X4), lhsT_scale=w_scl[n][:, wc],
+                                rhs=a_cod[nm][:, ac].bitcast(FP8X4), rhs_scale=a_scl[nm][:, ac], start=start, stop=stop)
+
+        def MX(n):
+            w, s = units[n]
+            for e in range(2):
+                key = (2 * s + e, GATE[w])
+                if OPENS[w]:
+                    acc[key] = pg.tile([P, B], F32, name="acc", tag="acc")
+                for g in range(2):
+                    mx_pass(acc[key][:], n, e, g, 0, B, OPENS[w] and g == 0, CLOSES[w] and g == 1)
+
+        tl = {}
+
+        def SR(m):
+            tl[(m, "r")] = ep.tile([P, B], F32, name="r")
+            nc.scalar.activation(out=tl[(m, "r")][:], in_=acc[(m, "r")][:], func=ACTF.Sigmoid, bias=bias_s[:, m:m + 1], scale=1.0)
+
+        def SZ(m):
+            tl[(m, "z")] = ep.tile([P, B], F32, name="z")
+            nc.scalar.activation(out=tl[(m, "z")][:], in_=acc[(m, "z")][:], func=ACTF.Sigmoid, bias=bias_s[:, 8 + m:9 + m], scale=1.0)
+
+        def TT(m):
+            tl[(m, "t")] = ep.tile([P, B], F32, name="t")
+            nc.vector.scalar_tensor_tensor(out=tl[(m, "t")][:], in0=acc[(m, "hn")][:], scalar=bias_f[:, 40 + m:41 + m],
+                                           in1=tl[(m, "r")][:], op0=ALU.add, op1=ALU.mult)
+
+        def UU(m):
+            nc.vector.tensor_tensor(out=tl[(m, "t")][:], in0=acc[(m, "in")][:], in1=tl[(m, "t")][:], op=ALU.add)
+
+        def TH(m):
+            tl[(m, "n")] = ep.tile([P, B], F32, name="n")
+            nc.scalar.activation(out=tl[(m, "n")][:], in_=tl[(m, "t")][:], func=ACTF.Tanh, bias=bias_f[:, 32 + m:33 + m], scale=1.0)
+
+        def DD(m):
+            s, e = divmod(m, 2)
+            g, u = divmod(s, 2)
+            h_t = a_grp["h"][:].rearrange("p (j g q t) -> p j g q t", j=4, g=2, t=4)[:, :, g, :, 2 * u + e]
+            tl[(m, "o")] = ep.tile([P, B], F32, name="o")
+            nc.vector.tensor_tensor(out=tl[(m, "o")][:].rearrange("p (j q) -> p j q", j=4), in0=h_t,
+                                    in1=tl[(m, "n")][:].rearrange("p (j q) -> p j q", j=4), op=ALU.subtract)
+
+        def EE(m, cols=slice(0, B)):
+            nc.vector.tensor_tensor(out=tl[(m, "o")][:, cols], in0=tl[(m, "z")][:, cols], in1=tl[(m, "o")][:, cols], op=ALU.mult)
+
+        def OO(m, cols=slice(0, B)):
+            nc.vector.tensor_tensor(out=tl[(m, "o")][:, cols], in0=tl[(m, "n")][:, cols], in1=tl[(m, "o")][:, cols], op=ALU.add)
+
+        o_sb = {}
+        out_v = out.rearrange("(q j) o -> q j o", j=4)
+
+        def OT(s, jh):
+            bank = pt.tile([P, 4, P], F32, name="tb", tag="tb")
+            for jj in range(2):
+                for e in range(2):
+                    j = 2 * jh + jj
+                    nc.tensor.transpose(bank[:, 2 * jj + e, :], tl[(2 * s + e, "o")][:, j * P:(j + 1) * P], ident[:])
+            banks[("o", s, jh)] = bank
+
+        def OE(s, jh, eng="v"):
+            if jh == 0:
+                o_sb[s] = osb.tile([P, 4, 256], F32, name="o_sb")
+            dst = o_sb[s][:, 2 * jh:2 * jh + 2, :].rearrange("q j (p e) -> q j p e", e=2)
+            copy_out(eng, dst, banks[("o", s, jh)].rearrange("q (j e) p -> q j p e", e=2))
+
+        def ST(s, js=slice(0, 4)):
+            nc.sync.dma_start(out=out_v[:, js, s * 256:(s + 1) * 256], in_=o_sb[s][:, js, :])
+
+        def tr_ev(n, e, eng="s"):
+            if n < 24:
+                TR(n, e)
+                EV(n, e, eng)
+
+        def qu(n):
+            if n < 24:
+                QU(n)
+
+        BIAS()
+        for j in range(4):
+            AT("x", j)
+            AE("x", j, "sv"[j % 2])
+            if j % 2 == 1:
+                AQ("x", j - 1)
+                AQ("x", j)
+        for n in range(2):
+            tr_ev(n, 0, "s")
+            tr_ev(n, 1, "v")
+            QU(n)
+        for j in range(2):
+            AT("h", j)
+            AE("h", j, "sv"[j % 2])
+        AQ("h", 0)
+        AQ("h", 1)
+        MX(0)
+        for j in range(2, 4):
+            AT("h", j)
+            AE("h", j, "sv"[j % 2])
+        tr_ev(2, 0, "s")
+        AQ("h", 2)
+        AQ("h", 3)
+        tr_ev(2, 1, "s")
+        QU(2)
+        MX(1)
+        tr_ev(3, 0, "s")
+        tr_ev(3, 1, "v")
+        QU(3)
+        MX(2)
+        SR(0)
+        SR(1)
+        for n in (4, 5):
+            tr_ev(n, 0, "s")
+            tr_ev(n, 1, "s")
+        MX(3)
+        TT(0)
+        QU(4)
+        TT(1)
+        UU(0)
+        QU(5)
+        UU(1)
+        tr_ev(6, 0)
+        TH(0)
+        tr_ev(6, 1)
+        TH(1)
+        tr_ev(7, 0)
+        tr_ev(7, 1)
+
+        for k in range(2, 11):
+            s, typ = divmod(k, 3)
+            a, b = 2 * s, 2 * s + 1
+            n0 = 2 * (k + 2)
+            MX(2 * k)
+            MX(2 * k + 1)
+            if typ == 0:
+                SR(a)
+                SR(b)
+                OO(a - 2)
+                qu(n0 - 2)
+                OO(b - 2)
+                qu(n0 - 1)
+                for n in (n0, n0 + 1):
+                    for e in range(2):
+                        tr_ev(n, e)
+            elif typ == 1:
+                TT(a)
+                TT(b)
+                qu(n0 - 2)
+                UU(a)
+                qu(n0 - 1)
+                UU(b)
+                tr_ev(n0, 0)
+                TH(a)
+                tr_ev(n0, 1)
+                TH(b)
+                tr_ev(n0 + 1, 0)
+                tr_ev(n0 + 1, 1)
+                OT(s - 1, 0)
+                OE(s - 1, 0, "s" if s == 3 else "v")
+            else:
+                DD(a)
+                qu(n0 - 2)
+                DD(b)
+                qu(n0 - 1)
+                SZ(a)
+                SZ(b)
+                if s > 0:
+                    OT(s - 1, 1)
+                    OE(s - 1, 1)
+                    ST(s - 1)
+                for n in (n0, n0 + 1):
+                    for e in range(2):
+                        tr_ev(n, e)
+                EE(a)
+                EE(b)
+
+        DD(6)
+        DD(7)
+        OT(2, 1)
+        OE(2, 1, "s")
+        ST(2)
+        for m in (6, 7):
+            tl[(m, "z")] = ep.tile([P, B], F32, name="z")
+        o_sb[3] = osb.tile([P, 4, 256], F32, name="o_sb")
+        for jh in range(2):
+            cols = slice(jh * 256, (jh + 1) * 256)
+            for e in range(2):
+                m = 6 + e
+                bank = pg.tile([P, 256], F32, name="acc", tag="acc")
+                for c, (n, g) in enumerate([(22, 0), (22, 1), (23, 0), (23, 1)]):
+                    mx_pass(bank[:], n, e, g, jh * 256, (jh + 1) * 256, c == 0, c == 3)
+                nc.scalar.activation(out=tl[(m, "z")][:, cols], in_=bank[:], func=ACTF.Sigmoid, bias=bias_s[:, 8 + m:9 + m], scale=1.0)
+            EE(6, cols)
+            EE(7, cols)
+            OO(6, cols)
+            OO(7, cols)
+        for jh in range(2):
+            OT(3, jh)
+            dst = o_sb[3][:, 2 * jh:2 * jh + 2, :].rearrange("q j (p e) -> q j p e", e=2)
+            copy_out("vs"[jh], dst, banks[("o", 3, jh)].rearrange("q (j e) p -> q j p e", e=2))
+            ST(3, slice(2 * jh, 2 * jh + 2))

@@ -45,14 +45,14 @@ def tile_gru_kernel(tc, x, hidden, Wir_w, Wir_b, Whr_w, Whr_b, Wiz_w, Wiz_b, Whz
         ep = ctx.enter_context(tc.tile_pool(name="ep", bufs=4))
         osb = ctx.enter_context(tc.tile_pool(name="osb", bufs=2))
         pt = ctx.enter_context(tc.psum_pool(name="pt", bufs=4))
-        pg = ctx.enter_context(tc.psum_pool(name="pg", bufs=4))
+        pg = ctx.enter_context(tc.psum_pool(name="pg", bufs=1))
 
+        ident = const.tile([P, P], F32, name="ident")
+        masks.make_identity(nc, ident[:])
         b_raw = const.tile([P, 2 * P], BF16, name="b_raw")
         nc.vector.memset(b_raw[:], 0.0)
         for v in range(6):
-            nc.scalar.dma_start(out=b_raw[4 * v:4 * v + 4, :], in_=biases[v].rearrange("(s c) -> s c", s=4))
-        ident = const.tile([P, P], F32, name="ident")
-        masks.make_identity(nc, ident[:])
+            nc.gpsimd.dma_start(out=b_raw[4 * v:4 * v + 4, :], in_=biases[v].rearrange("(s c) -> s c", s=4))
         warm = const.tile([P, 1], F32, name="warm")
         nc.vector.memset(warm[:], 0.0)
         nc.scalar.activation(out=warm[:], in_=warm[:], func=ACTF.Sigmoid)
@@ -66,8 +66,8 @@ def tile_gru_kernel(tc, x, hidden, Wir_w, Wir_b, Whr_w, Whr_b, Wiz_w, Wiz_b, Whz
 
         def load_act(nm, src):
             view = src.rearrange("(q j) k -> q (j k)", j=4)
-            for half in range(2):
-                cols = slice(half * 2 * K, (half + 1) * 2 * K)
+            for j in range(4):
+                cols = slice(j * K, (j + 1) * K)
                 nc.sync.dma_start(out=act_raw[nm][:, cols], in_=view[:, cols])
 
         def load_w(n):
@@ -152,12 +152,16 @@ def tile_gru_kernel(tc, x, hidden, Wir_w, Wir_b, Whr_w, Whr_b, Wiz_w, Wiz_b, Whz
             nc.tensor.matmul_mx(out=bank, lhsT=w_cod[n][:, wc].bitcast(FP8X4), lhsT_scale=w_scl[n][:, wc],
                                 rhs=a_cod[nm][:, ac].bitcast(FP8X4), rhs_scale=a_scl[nm][:, ac], start=start, stop=stop)
 
+        def bank_tag(w, s, e):
+            first = (GATE[w] in ("hn", "z")) or (s == 0 and GATE[w] == "r")
+            return "acc_%s%d" % ("a" if first else "b", e)
+
         def MX(n):
             w, s = units[n]
             for e in range(2):
                 key = (2 * s + e, GATE[w])
                 if OPENS[w]:
-                    acc[key] = pg.tile([P, B], F32, name="acc", tag="acc")
+                    acc[key] = pg.tile([P, B], F32, name="acc", tag=bank_tag(w, s, e))
                 for g in range(2):
                     mx_pass(acc[key][:], n, e, g, 0, B, OPENS[w] and g == 0, CLOSES[w] and g == 1)
 
@@ -226,7 +230,6 @@ def tile_gru_kernel(tc, x, hidden, Wir_w, Wir_b, Whr_w, Whr_b, Wiz_w, Wiz_b, Whz
             if n < 24:
                 QU(n)
 
-        BIAS()
         for j in range(4):
             AT("x", j)
             AE("x", j, "sv"[j % 2])
@@ -254,6 +257,7 @@ def tile_gru_kernel(tc, x, hidden, Wir_w, Wir_b, Whr_w, Whr_b, Wiz_w, Wiz_b, Whz
         MX(1)
         tr_ev(3, 0, "s")
         tr_ev(3, 1, "v")
+        BIAS()
         QU(3)
         MX(2)
         SR(0)
@@ -275,7 +279,7 @@ def tile_gru_kernel(tc, x, hidden, Wir_w, Wir_b, Whr_w, Whr_b, Wiz_w, Wiz_b, Whz
         tr_ev(7, 0)
         tr_ev(7, 1)
 
-        for k in range(2, 11):
+        for k in range(2, 10):
             s, typ = divmod(k, 3)
             a, b = 2 * s, 2 * s + 1
             n0 = 2 * (k + 2)
@@ -305,29 +309,41 @@ def tile_gru_kernel(tc, x, hidden, Wir_w, Wir_b, Whr_w, Whr_b, Wiz_w, Wiz_b, Whz
                 tr_ev(n0 + 1, 0)
                 tr_ev(n0 + 1, 1)
                 OT(s - 1, 0)
-                OE(s - 1, 0, "s" if s == 3 else "v")
+                OE(s - 1, 0)
             else:
                 DD(a)
                 qu(n0 - 2)
                 DD(b)
                 qu(n0 - 1)
                 SZ(a)
+                tr_ev(n0, 0)
                 SZ(b)
+                tr_ev(n0, 1)
+                tr_ev(n0 + 1, 0)
+                tr_ev(n0 + 1, 1)
                 if s > 0:
                     OT(s - 1, 1)
                     OE(s - 1, 1)
                     ST(s - 1)
-                for n in (n0, n0 + 1):
-                    for e in range(2):
-                        tr_ev(n, e)
                 EE(a)
                 EE(b)
 
+        MX(20)
+        MX(21)
+        QU(22)
+        TT(6)
+        QU(23)
+        TT(7)
+        UU(6)
+        UU(7)
+        for jh in range(2):
+            OT(2, jh)
+            OE(2, jh, "s")
+        ST(2)
+        TH(6)
+        TH(7)
         DD(6)
         DD(7)
-        OT(2, 1)
-        OE(2, 1, "s")
-        ST(2)
         for m in (6, 7):
             tl[(m, "z")] = ep.tile([P, B], F32, name="z")
         o_sb[3] = osb.tile([P, 4, 256], F32, name="o_sb")
@@ -335,7 +351,7 @@ def tile_gru_kernel(tc, x, hidden, Wir_w, Wir_b, Whr_w, Whr_b, Wiz_w, Wiz_b, Whz
             cols = slice(jh * 256, (jh + 1) * 256)
             for e in range(2):
                 m = 6 + e
-                bank = pg.tile([P, 256], F32, name="acc", tag="acc")
+                bank = pg.tile([P, 256], F32, name="acc", tag="acc_%s%d" % ("ab"[jh], e))
                 for c, (n, g) in enumerate([(22, 0), (22, 1), (23, 0), (23, 1)]):
                     mx_pass(bank[:], n, e, g, jh * 256, (jh + 1) * 256, c == 0, c == 3)
                 nc.scalar.activation(out=tl[(m, "z")][:, cols], in_=bank[:], func=ACTF.Sigmoid, bias=bias_s[:, 8 + m:9 + m], scale=1.0)

@@ -118,11 +118,14 @@ def tile_gru_kernel(tc, x, hidden, Wir_w, Wir_b, Whr_w, Whr_b, Wiz_w, Wiz_b, Whz
         bias_f = const.tile([P, 64], F32, name="bias_f")
         bias_s = const.tile([P, 16], F32, name="bias_s")
 
-        def BIAS():
+        bias_w = const.tile([P, 32], F32, name="bias_w")
+
+        def BIAS_T():
             bank = pt.tile([P, 4, P], F32, name="tb", tag="tb")
             nc.tensor.transpose(bank[:, 0, :], b_raw[:].bitcast(F32), ident[:])
-            bias_w = const.tile([P, 32], F32, name="bias_w")
             nc.vector.tensor_copy(out=bias_w[:], in_=bank[:, 0, 0:32])
+
+        def BIAS_V():
             nc.vector.tensor_copy(out=bias_f[:], in_=bias_w[:].bitcast(BF16))
             nc.vector.tensor_tensor(out=bias_s[:, 0:8], in0=bias_f[:, 0:8], in1=bias_f[:, 8:16], op=ALU.add)
             nc.vector.tensor_tensor(out=bias_s[:, 8:16], in0=bias_f[:, 16:24], in1=bias_f[:, 24:32], op=ALU.add)
@@ -253,11 +256,12 @@ def tile_gru_kernel(tc, x, hidden, Wir_w, Wir_b, Whr_w, Whr_b, Wiz_w, Wiz_b, Whz
         AQ("h", 2)
         AQ("h", 3)
         tr_ev(2, 1, "s")
+        BIAS_T()
         QU(2)
+        BIAS_V()
         MX(1)
         tr_ev(3, 0, "s")
         tr_ev(3, 1, "v")
-        BIAS()
         QU(3)
         MX(2)
         SR(0)
@@ -266,18 +270,18 @@ def tile_gru_kernel(tc, x, hidden, Wir_w, Wir_b, Whr_w, Whr_b, Wiz_w, Wiz_b, Whz
             tr_ev(n, 0, "s")
             tr_ev(n, 1, "s")
         MX(3)
-        TT(0)
         QU(4)
+        TT(0)
+        QU(5)
         TT(1)
         UU(0)
-        QU(5)
         UU(1)
         tr_ev(6, 0)
-        TH(0)
         tr_ev(6, 1)
-        TH(1)
         tr_ev(7, 0)
         tr_ev(7, 1)
+        TH(0)
+        TH(1)
 
         for k in range(2, 10):
             s, typ = divmod(k, 3)

@@ -128,7 +128,8 @@ def tile_gru_kernel(tc, x, hidden, Wir_w, Wir_b, Whr_w, Whr_b, Wiz_w, Wiz_b, Whz
         def BIAS_V():
             nc.vector.tensor_copy(out=bias_f[:], in_=bias_w[:].bitcast(BF16))
             nc.vector.tensor_tensor(out=bias_s[:, 0:8], in0=bias_f[:, 0:8], in1=bias_f[:, 8:16], op=ALU.add)
-            nc.vector.tensor_tensor(out=bias_s[:, 8:16], in0=bias_f[:, 16:24], in1=bias_f[:, 24:32], op=ALU.add)
+            nc.vector.scalar_tensor_tensor(out=bias_s[:, 8:16], in0=bias_f[:, 16:24], scalar=-1.0, in1=bias_f[:, 24:32],
+                                           op0=ALU.mult, op1=ALU.subtract)
 
         w_grp, w_cod, w_scl = {}, {}, {}
 
@@ -176,7 +177,7 @@ def tile_gru_kernel(tc, x, hidden, Wir_w, Wir_b, Whr_w, Whr_b, Wiz_w, Wiz_b, Whz
 
         def SZ(m):
             tl[(m, "z")] = ep.tile([P, B], F32, name="z")
-            nc.scalar.activation(out=tl[(m, "z")][:], in_=acc[(m, "z")][:], func=ACTF.Sigmoid, bias=bias_s[:, 8 + m:9 + m], scale=1.0)
+            nc.scalar.activation(out=tl[(m, "z")][:], in_=acc[(m, "z")][:], func=ACTF.Sigmoid, bias=bias_s[:, 8 + m:9 + m], scale=-1.0)
 
         def TT(m):
             tl[(m, "t")] = ep.tile([P, B], F32, name="t")
@@ -201,9 +202,6 @@ def tile_gru_kernel(tc, x, hidden, Wir_w, Wir_b, Whr_w, Whr_b, Wiz_w, Wiz_b, Whz
         def EE(m, cols=slice(0, B)):
             nc.vector.tensor_tensor(out=tl[(m, "o")][:, cols], in0=tl[(m, "z")][:, cols], in1=tl[(m, "o")][:, cols], op=ALU.mult)
 
-        def OO(m, cols=slice(0, B)):
-            nc.vector.tensor_tensor(out=tl[(m, "o")][:, cols], in0=tl[(m, "n")][:, cols], in1=tl[(m, "o")][:, cols], op=ALU.add)
-
         o_sb = {}
         out_v = out.rearrange("(q j) o -> q j o", j=4)
 
@@ -215,11 +213,14 @@ def tile_gru_kernel(tc, x, hidden, Wir_w, Wir_b, Whr_w, Whr_b, Wiz_w, Wiz_b, Whz
                     nc.tensor.transpose(bank[:, 2 * jj + e, :], tl[(2 * s + e, "o")][:, j * P:(j + 1) * P], ident[:])
             banks[("o", s, jh)] = bank
 
-        def OE(s, jh, eng="v"):
+        def OE(s, jh):
             if jh == 0:
                 o_sb[s] = osb.tile([P, 4, 256], F32, name="o_sb")
-            dst = o_sb[s][:, 2 * jh:2 * jh + 2, :].rearrange("q j (p e) -> q j p e", e=2)
-            copy_out(eng, dst, banks[("o", s, jh)].rearrange("q (j e) p -> q j p e", e=2))
+            js = slice(2 * jh, 2 * jh + 2)
+            h_t = act_raw["h"][:].rearrange("q (j k) -> q j k", j=4)[:, js, s * 256:(s + 1) * 256]
+            nc.vector.tensor_tensor(out=o_sb[s][:, js, :].rearrange("q j (p e) -> q j p e", e=2),
+                                    in0=h_t.rearrange("q j (p e) -> q j p e", e=2),
+                                    in1=banks[("o", s, jh)].rearrange("q (j e) p -> q j p e", e=2), op=ALU.subtract)
 
         def ST(s, js=slice(0, 4)):
             nc.sync.dma_start(out=out_v[:, js, s * 256:(s + 1) * 256], in_=o_sb[s][:, js, :])
@@ -256,13 +257,13 @@ def tile_gru_kernel(tc, x, hidden, Wir_w, Wir_b, Whr_w, Whr_b, Wiz_w, Wiz_b, Whz
         AQ("h", 2)
         AQ("h", 3)
         tr_ev(2, 1, "s")
-        BIAS_T()
         QU(2)
-        BIAS_V()
         MX(1)
         tr_ev(3, 0, "s")
         tr_ev(3, 1, "v")
+        BIAS_T()
         QU(3)
+        BIAS_V()
         MX(2)
         SR(0)
         SR(1)
@@ -292,9 +293,7 @@ def tile_gru_kernel(tc, x, hidden, Wir_w, Wir_b, Whr_w, Whr_b, Wiz_w, Wiz_b, Whz
             if typ == 0:
                 SR(a)
                 SR(b)
-                OO(a - 2)
                 qu(n0 - 2)
-                OO(b - 2)
                 qu(n0 - 1)
                 for n in (n0, n0 + 1):
                     for e in range(2):
@@ -342,7 +341,7 @@ def tile_gru_kernel(tc, x, hidden, Wir_w, Wir_b, Whr_w, Whr_b, Wiz_w, Wiz_b, Whz
         UU(7)
         for jh in range(2):
             OT(2, jh)
-            OE(2, jh, "s")
+            OE(2, jh)
         ST(2)
         TH(6)
         TH(7)
@@ -350,7 +349,6 @@ def tile_gru_kernel(tc, x, hidden, Wir_w, Wir_b, Whr_w, Whr_b, Wiz_w, Wiz_b, Whz
         DD(7)
         for m in (6, 7):
             tl[(m, "z")] = ep.tile([P, B], F32, name="z")
-        o_sb[3] = osb.tile([P, 4, 256], F32, name="o_sb")
         for jh in range(2):
             cols = slice(jh * 256, (jh + 1) * 256)
             for e in range(2):
@@ -358,13 +356,10 @@ def tile_gru_kernel(tc, x, hidden, Wir_w, Wir_b, Whr_w, Whr_b, Wiz_w, Wiz_b, Whz
                 bank = pg.tile([P, 256], F32, name="acc", tag="acc_%s%d" % ("ab"[jh], e))
                 for c, (n, g) in enumerate([(22, 0), (22, 1), (23, 0), (23, 1)]):
                     mx_pass(bank[:], n, e, g, jh * 256, (jh + 1) * 256, c == 0, c == 3)
-                nc.scalar.activation(out=tl[(m, "z")][:, cols], in_=bank[:], func=ACTF.Sigmoid, bias=bias_s[:, 8 + m:9 + m], scale=1.0)
+                nc.scalar.activation(out=tl[(m, "z")][:, cols], in_=bank[:], func=ACTF.Sigmoid, bias=bias_s[:, 8 + m:9 + m], scale=-1.0)
             EE(6, cols)
             EE(7, cols)
-            OO(6, cols)
-            OO(7, cols)
         for jh in range(2):
             OT(3, jh)
-            dst = o_sb[3][:, 2 * jh:2 * jh + 2, :].rearrange("q j (p e) -> q j p e", e=2)
-            copy_out("vs"[jh], dst, banks[("o", 3, jh)].rearrange("q (j e) p -> q j p e", e=2))
+            OE(3, jh)
             ST(3, slice(2 * jh, 2 * jh + 2))

@@ -53,6 +53,8 @@ def tile_gru_kernel(tc, x, hidden, Wir_w, Wir_b, Whr_w, Whr_b, Wiz_w, Wiz_b, Whz
         nc.vector.memset(b_raw[:], 0.0)
         for v in range(6):
             nc.gpsimd.dma_start(out=b_raw[4 * v:4 * v + 4, :], in_=biases[v].rearrange("(s c) -> s c", s=4))
+        idle = const.tile([P, 512], BF16, name="idle")
+        nc.vector.memset(idle[:], 0.0)
         warm = const.tile([P, 1], F32, name="warm")
         nc.vector.memset(warm[:], 0.0)
         nc.scalar.activation(out=warm[:], in_=warm[:], func=ACTF.Sigmoid)
@@ -89,6 +91,11 @@ def tile_gru_kernel(tc, x, hidden, Wir_w, Wir_b, Whr_w, Whr_b, Wiz_w, Wiz_b, Whz
             for c in range(4):
                 nc.tensor.transpose(bank[:, c, :], words[:, c * P:(c + 1) * P], ident[:])
             banks[key] = bank
+
+        def dummies(n):
+            bank = pg.tile([P, B], F32, name="acc", tag="acc_b1")
+            for c in range(n):
+                nc.tensor.matmul(bank[:], idle[:, 0:P], idle[:], start=True, stop=True)
 
         def copy_out(eng, dst, src):
             if eng == "s":
@@ -234,15 +241,18 @@ def tile_gru_kernel(tc, x, hidden, Wir_w, Wir_b, Whr_w, Whr_b, Wiz_w, Wiz_b, Whz
             if n < 24:
                 QU(n)
 
+        dummies(5)
         for j in range(4):
             AT("x", j)
             AE("x", j, "sv"[j % 2])
             if j % 2 == 1:
+                dummies(2)
                 AQ("x", j - 1)
                 AQ("x", j)
         for n in range(2):
             tr_ev(n, 0, "s")
             tr_ev(n, 1, "v")
+            dummies(2)
             QU(n)
         for j in range(2):
             AT("h", j)

@@ -17,15 +17,12 @@ K = 1024
 H = 1024
 FLOPS = 2 * B * K * H * 6
 
-PINNED = True
-
 IR, HR, HN, IN, IZ, HZ = 0, 1, 2, 3, 4, 5
 SRC = ["x", "h", "h", "x", "x", "h"]
 GATE = ["r", "r", "hn", "in", "z", "z"]
-OPENS = [True, False, True, True, True, False]
-CLOSES = [False, True, True, True, False, True]
-ORDER0 = [IR, IN, HR, HN, IZ, HZ]
-ORDER = [IR, HR, HN, IN, IZ, HZ]
+UNITS = ([(w, 0) for w in (IR, IN, HR, HN, IZ, HZ)]
+         + [(w, s) for s in range(1, 4) for w in (IR, HR, HN, IN)]
+         + [(w, s) for s in range(1, 4) for w in (IZ, HZ)])
 
 
 def tile_gru_kernel(tc, x, hidden, Wir_w, Wir_b, Whr_w, Whr_b, Wiz_w, Wiz_b, Whz_w, Whz_b,
@@ -33,28 +30,25 @@ def tile_gru_kernel(tc, x, hidden, Wir_w, Wir_b, Whr_w, Whr_b, Wiz_w, Wiz_b, Whz
     nc = tc.nc
     weights = [Wir_w, Whr_w, Whn_w, Win_w, Wiz_w, Whz_w]
     biases = [Wir_b, Whr_b, Wiz_b, Whz_b, Win_b, Whn_b]
-    units = [(w, 0) for w in ORDER0] + [(w, s) for s in range(1, 4) for w in ORDER]
     with ExitStack() as ctx:
-        if PINNED:
-            ctx.enter_context(tc.manual_schedule())
+        ctx.enter_context(tc.manual_schedule())
         const = ctx.enter_context(tc.tile_pool(name="const", bufs=1))
         raw = ctx.enter_context(tc.tile_pool(name="raw", bufs=1))
         keep = ctx.enter_context(tc.tile_pool(name="keep", bufs=1))
         grp = ctx.enter_context(tc.tile_pool(name="grp", bufs=4))
-        cod = ctx.enter_context(tc.tile_pool(name="cod", bufs=6))
+        cod = ctx.enter_context(tc.tile_pool(name="cod", bufs=5))
         ep = ctx.enter_context(tc.tile_pool(name="ep", bufs=4))
+        eph = ctx.enter_context(tc.tile_pool(name="eph", bufs=6))
         osb = ctx.enter_context(tc.tile_pool(name="osb", bufs=2))
         pt = ctx.enter_context(tc.psum_pool(name="pt", bufs=4))
         pg = ctx.enter_context(tc.psum_pool(name="pg", bufs=1))
 
-        ident = const.tile([P, P], F32, name="ident")
-        masks.make_identity(nc, ident[:])
-        b_raw = const.tile([P, 2 * P], BF16, name="b_raw")
-        nc.vector.memset(b_raw[:], 0.0)
-        for v in range(6):
-            nc.gpsimd.dma_start(out=b_raw[4 * v:4 * v + 4, :], in_=biases[v].rearrange("(s c) -> s c", s=4))
         idle = const.tile([P, 512], BF16, name="idle")
         nc.vector.memset(idle[:], 0.0)
+        b_raw = const.tile([P, 2 * P], BF16, name="b_raw")
+        nc.vector.memset(b_raw[:], 0.0)
+        ident = const.tile([P, P], F32, name="ident")
+        masks.make_identity(nc, ident[:])
         warm = const.tile([P, 1], F32, name="warm")
         nc.vector.memset(warm[:], 0.0)
         nc.scalar.activation(out=warm[:], in_=warm[:], func=ACTF.Sigmoid)
@@ -72,17 +66,24 @@ def tile_gru_kernel(tc, x, hidden, Wir_w, Wir_b, Whr_w, Whr_b, Wiz_w, Wiz_b, Whz
                 cols = slice(j * K, (j + 1) * K)
                 nc.sync.dma_start(out=act_raw[nm][:, cols], in_=view[:, cols])
 
-        def load_w(n):
-            w, s = units[n]
-            view = weights[w].rearrange("(s q e) k -> s q (e k)", s=4, e=2)
-            nc.sync.dma_start(out=w_raw[n][:], in_=view[s])
+        def load_w(n, parts):
+            w, s = UNITS[n]
+            view = weights[w].rearrange("(s q e) k -> s q (e k)", s=4, e=2)[s]
+            width = 2 * K // parts
+            for c in range(parts):
+                cols = slice(c * width, (c + 1) * width)
+                nc.sync.dma_start(out=w_raw[n][:, cols], in_=view[:, cols])
 
         load_act("x", x)
-        load_w(0)
-        load_w(1)
+        load_w(0, 2)
+        load_w(1, 2)
         load_act("h", hidden)
-        for n in range(2, 24):
-            load_w(n)
+        load_w(2, 1)
+        load_w(3, 1)
+        for v in range(6):
+            nc.sync.dma_start(out=b_raw[4 * v:4 * v + 4, :], in_=biases[v].rearrange("(s c) -> s c", s=4))
+        for n in range(4, 24):
+            load_w(n, 1)
 
         banks = {}
 
@@ -124,7 +125,6 @@ def tile_gru_kernel(tc, x, hidden, Wir_w, Wir_b, Whr_w, Whr_b, Wiz_w, Wiz_b, Whz
 
         bias_f = const.tile([P, 64], F32, name="bias_f")
         bias_s = const.tile([P, 16], F32, name="bias_s")
-
         bias_w = const.tile([P, 32], F32, name="bias_w")
 
         def BIAS_T():
@@ -155,44 +155,48 @@ def tile_gru_kernel(tc, x, hidden, Wir_w, Wir_b, Whr_w, Whr_b, Wiz_w, Wiz_b, Whz
             nc.vector.quantize_mx(out=w_cod[n][:].bitcast(FP8X4), scales=w_scl[n][:], in_=w_grp[n][:])
 
         acc = {}
+        passes = {}
 
-        def mx_pass(bank, n, e, g, c0, c1, start, stop):
-            nm = SRC[units[n][0]]
-            wc = slice(e * 256 + g * P, e * 256 + (g + 1) * P)
-            ac = slice(g * B + c0, g * B + c1)
-            nc.tensor.matmul_mx(out=bank, lhsT=w_cod[n][:, wc].bitcast(FP8X4), lhsT_scale=w_scl[n][:, wc],
-                                rhs=a_cod[nm][:, ac].bitcast(FP8X4), rhs_scale=a_scl[nm][:, ac], start=start, stop=stop)
+        def pair_of(gate, s):
+            if s == 0:
+                return "b" if gate == "in" else "a"
+            return "ab"[s % 2] if gate in ("r", "in") else "ba"[s % 2]
 
-        def bank_tag(w, s, e):
-            first = (GATE[w] in ("hn", "z")) or (s == 0 and GATE[w] == "r")
-            return "acc_%s%d" % ("a" if first else "b", e)
-
-        def MX(n):
-            w, s = units[n]
-            for e in range(2):
-                key = (2 * s + e, GATE[w])
-                if OPENS[w]:
-                    acc[key] = pg.tile([P, B], F32, name="acc", tag=bank_tag(w, s, e))
+        def MX(n, es=(0, 1), c0=0, c1=B):
+            w, s = UNITS[n]
+            nm, gate = SRC[w], GATE[w]
+            total = 2 if gate in ("hn", "in") else 4
+            for e in es:
+                key = (2 * s + e, gate, c0)
+                if key not in acc:
+                    acc[key] = pg.tile([P, c1 - c0], F32, name="acc", tag="acc_%s%d" % (pair_of(gate, s if c0 == 0 else s - 1), e))
+                    passes[key] = 0
                 for g in range(2):
-                    mx_pass(acc[key][:], n, e, g, 0, B, OPENS[w] and g == 0, CLOSES[w] and g == 1)
+                    wc = slice(e * 256 + g * P, e * 256 + (g + 1) * P)
+                    ac = slice(g * B + c0, g * B + c1)
+                    passes[key] += 1
+                    nc.tensor.matmul_mx(out=acc[key][:], lhsT=w_cod[n][:, wc].bitcast(FP8X4), lhsT_scale=w_scl[n][:, wc],
+                                        rhs=a_cod[nm][:, ac].bitcast(FP8X4), rhs_scale=a_scl[nm][:, ac],
+                                        start=passes[key] == 1, stop=passes[key] == total)
 
         tl = {}
 
         def SR(m):
             tl[(m, "r")] = ep.tile([P, B], F32, name="r")
-            nc.scalar.activation(out=tl[(m, "r")][:], in_=acc[(m, "r")][:], func=ACTF.Sigmoid, bias=bias_s[:, m:m + 1], scale=1.0)
+            nc.scalar.activation(out=tl[(m, "r")][:], in_=acc[(m, "r", 0)][:], func=ACTF.Sigmoid, bias=bias_s[:, m:m + 1], scale=1.0)
 
-        def SZ(m):
-            tl[(m, "z")] = ep.tile([P, B], F32, name="z")
-            nc.scalar.activation(out=tl[(m, "z")][:], in_=acc[(m, "z")][:], func=ACTF.Sigmoid, bias=bias_s[:, 8 + m:9 + m], scale=-1.0)
+        def SZ(m, c0=0, c1=B):
+            if (m, "z") not in tl:
+                tl[(m, "z")] = ep.tile([P, B], F32, name="z")
+            nc.scalar.activation(out=tl[(m, "z")][:, c0:c1], in_=acc[(m, "z", c0)][:], func=ACTF.Sigmoid, bias=bias_s[:, 8 + m:9 + m], scale=-1.0)
 
         def TT(m):
             tl[(m, "t")] = ep.tile([P, B], F32, name="t")
-            nc.vector.scalar_tensor_tensor(out=tl[(m, "t")][:], in0=acc[(m, "hn")][:], scalar=bias_f[:, 40 + m:41 + m],
+            nc.vector.scalar_tensor_tensor(out=tl[(m, "t")][:], in0=acc[(m, "hn", 0)][:], scalar=bias_f[:, 40 + m:41 + m],
                                            in1=tl[(m, "r")][:], op0=ALU.add, op1=ALU.mult)
 
         def UU(m):
-            nc.vector.tensor_tensor(out=tl[(m, "t")][:], in0=acc[(m, "in")][:], in1=tl[(m, "t")][:], op=ALU.add)
+            nc.vector.tensor_tensor(out=tl[(m, "t")][:], in0=acc[(m, "in", 0)][:], in1=tl[(m, "t")][:], op=ALU.add)
 
         def TH(m):
             tl[(m, "n")] = ep.tile([P, B], F32, name="n")
@@ -202,11 +206,12 @@ def tile_gru_kernel(tc, x, hidden, Wir_w, Wir_b, Whr_w, Whr_b, Wiz_w, Wiz_b, Whz
             s, e = divmod(m, 2)
             g, u = divmod(s, 2)
             h_t = a_grp["h"][:].rearrange("p (j g q t) -> p j g q t", j=4, g=2, t=4)[:, :, g, :, 2 * u + e]
-            tl[(m, "o")] = ep.tile([P, B], F32, name="o")
+            tl[(m, "o")] = eph.tile([P, B], F32, name="o")
             nc.vector.tensor_tensor(out=tl[(m, "o")][:].rearrange("p (j q) -> p j q", j=4), in0=h_t,
                                     in1=tl[(m, "n")][:].rearrange("p (j q) -> p j q", j=4), op=ALU.subtract)
 
-        def EE(m, cols=slice(0, B)):
+        def EE(m, c0=0, c1=B):
+            cols = slice(c0, c1)
             nc.vector.tensor_tensor(out=tl[(m, "o")][:, cols], in0=tl[(m, "z")][:, cols], in1=tl[(m, "o")][:, cols], op=ALU.mult)
 
         o_sb = {}
@@ -229,147 +234,168 @@ def tile_gru_kernel(tc, x, hidden, Wir_w, Wir_b, Whr_w, Whr_b, Wiz_w, Wiz_b, Whz
                                     in0=h_t.rearrange("q j (p e) -> q j p e", e=2),
                                     in1=banks[("o", s, jh)].rearrange("q (j e) p -> q j p e", e=2), op=ALU.subtract)
 
-        def ST(s, js=slice(0, 4)):
+        def ST(s, jh):
+            js = slice(2 * jh, 2 * jh + 2)
             nc.sync.dma_start(out=out_v[:, js, s * 256:(s + 1) * 256], in_=o_sb[s][:, js, :])
 
         def tr_ev(n, e, eng="s"):
-            if n < 24:
-                TR(n, e)
-                EV(n, e, eng)
-
-        def qu(n):
-            if n < 24:
-                QU(n)
+            TR(n, e)
+            EV(n, e, eng)
 
         dummies(5)
         for j in range(4):
             AT("x", j)
-            AE("x", j, "sv"[j % 2])
-            if j % 2 == 1:
+            AE("x", j, "s")
+            if j == 3:
                 dummies(2)
-                AQ("x", j - 1)
-                AQ("x", j)
-        for n in range(2):
-            tr_ev(n, 0, "s")
-            tr_ev(n, 1, "v")
-            dummies(2)
-            QU(n)
-        for j in range(2):
-            AT("h", j)
-            AE("h", j, "sv"[j % 2])
-        AQ("h", 0)
-        AQ("h", 1)
+            AQ("x", j)
+        tr_ev(0, 0, "s")
+        tr_ev(0, 1, "v")
+        dummies(2)
+        QU(0)
+        tr_ev(1, 0, "s")
+        tr_ev(1, 1, "s")
+        AT("h", 0)
+        AE("h", 0, "v")
         MX(0)
-        for j in range(2, 4):
+        QU(1)
+        AQ("h", 0)
+        for j in range(1, 4):
             AT("h", j)
-            AE("h", j, "sv"[j % 2])
-        tr_ev(2, 0, "s")
+            AE("h", j, "vs"[j % 2])
+        AQ("h", 1)
+        tr_ev(2, 0, "v")
         AQ("h", 2)
-        AQ("h", 3)
         tr_ev(2, 1, "s")
+        AQ("h", 3)
         QU(2)
         MX(1)
         tr_ev(3, 0, "s")
-        tr_ev(3, 1, "v")
+        tr_ev(3, 1, "s")
         BIAS_T()
         QU(3)
         BIAS_V()
         MX(2)
         SR(0)
         SR(1)
-        for n in (4, 5):
-            tr_ev(n, 0, "s")
-            tr_ev(n, 1, "s")
+        tr_ev(4, 0, "v")
+        tr_ev(4, 1)
+        tr_ev(5, 0)
+        tr_ev(5, 1)
         MX(3)
         QU(4)
         TT(0)
-        QU(5)
         TT(1)
+        QU(5)
         UU(0)
         UU(1)
-        tr_ev(6, 0)
-        tr_ev(6, 1)
-        tr_ev(7, 0)
-        tr_ev(7, 1)
+        for n in (6, 7):
+            tr_ev(n, 0)
+            tr_ev(n, 1)
         TH(0)
         TH(1)
+        MX(4)
+        MX(5)
+        DD(0)
+        QU(6)
+        DD(1)
+        QU(7)
+        SZ(0)
+        tr_ev(8, 0)
+        SZ(1)
+        tr_ev(8, 1)
+        tr_ev(9, 0)
+        tr_ev(9, 1)
+        EE(0)
+        EE(1)
 
-        for k in range(2, 10):
-            s, typ = divmod(k, 3)
+        for s in range(1, 4):
             a, b = 2 * s, 2 * s + 1
-            n0 = 2 * (k + 2)
-            MX(2 * k)
-            MX(2 * k + 1)
-            if typ == 0:
-                SR(a)
-                SR(b)
-                qu(n0 - 2)
-                qu(n0 - 1)
-                for n in (n0, n0 + 1):
-                    for e in range(2):
-                        tr_ev(n, e)
-            elif typ == 1:
-                TT(a)
-                TT(b)
-                qu(n0 - 2)
-                UU(a)
-                qu(n0 - 1)
-                UU(b)
-                tr_ev(n0, 0)
-                TH(a)
-                tr_ev(n0, 1)
-                TH(b)
-                tr_ev(n0 + 1, 0)
-                tr_ev(n0 + 1, 1)
-                OT(s - 1, 0)
-                OE(s - 1, 0)
-            else:
-                DD(a)
-                qu(n0 - 2)
-                DD(b)
-                qu(n0 - 1)
-                SZ(a)
-                tr_ev(n0, 0)
-                SZ(b)
-                tr_ev(n0, 1)
-                tr_ev(n0 + 1, 0)
-                tr_ev(n0 + 1, 1)
-                if s > 0:
-                    OT(s - 1, 1)
-                    OE(s - 1, 1)
-                    ST(s - 1)
-                EE(a)
-                EE(b)
+            n = 4 * s + 2
+            MX(n)
+            MX(n + 1)
+            if s > 1:
+                DD(a - 2)
+            QU(n + 2)
+            if s > 1:
+                DD(b - 2)
+            QU(n + 3)
+            SR(a)
+            tr_ev(n + 4, 0)
+            SR(b)
+            tr_ev(n + 4, 1)
+            tr_ev(n + 5, 0)
+            tr_ev(n + 5, 1, "v")
+            if s == 1:
+                OT(0, 0)
+                OE(0, 0)
+                ST(0, 0)
+            n += 2
+            MX(n)
+            MX(n + 1)
+            TT(a)
+            TT(b)
+            QU(n + 2)
+            UU(a)
+            QU(n + 3)
+            UU(b)
+            tr_ev(n + 4, 0)
+            TH(a)
+            tr_ev(n + 4, 1)
+            TH(b)
+            tr_ev(n + 5, 0)
+            tr_ev(n + 5, 1)
+            if s == 1:
+                OT(0, 1)
+                OE(0, 1)
+                ST(0, 1)
 
+        MX(18)
+        MX(19)
+        DD(6)
+        QU(20)
+        DD(7)
+        QU(21)
+        SZ(2)
+        tr_ev(22, 0)
+        EE(2)
+        SZ(3)
+        tr_ev(22, 1)
+        tr_ev(23, 0)
+        tr_ev(23, 1, "v")
+        EE(3)
+        QU(22)
         MX(20)
         MX(21)
-        QU(22)
-        TT(6)
         QU(23)
-        TT(7)
-        UU(6)
-        UU(7)
+        OT(1, 0)
+        OT(1, 1)
+        SZ(4)
+        SZ(5)
         for jh in range(2):
-            OT(2, jh)
+            OE(1, jh)
+            ST(1, jh)
+        EE(4)
+        EE(5)
+        MX(22, (0,))
+        MX(23, (0,))
+        SZ(6)
+        MX(22, (1,), 0, 256)
+        MX(23, (1,), 0, 256)
+        OT(2, 0)
+        OT(2, 1)
+        MX(22, (1,), 256, 512)
+        MX(23, (1,), 256, 512)
+        SZ(7, 0, 256)
+        SZ(7, 256, 512)
+        EE(6)
+        EE(7, 0, 256)
+        OT(3, 0)
+        for jh in range(2):
             OE(2, jh)
-        ST(2)
-        TH(6)
-        TH(7)
-        DD(6)
-        DD(7)
-        for m in (6, 7):
-            tl[(m, "z")] = ep.tile([P, B], F32, name="z")
+            ST(2, jh)
+        EE(7, 256, 512)
+        OT(3, 1)
         for jh in range(2):
-            cols = slice(jh * 256, (jh + 1) * 256)
-            for e in range(2):
-                m = 6 + e
-                bank = pg.tile([P, 256], F32, name="acc", tag="acc_%s%d" % ("ab"[jh], e))
-                for c, (n, g) in enumerate([(22, 0), (22, 1), (23, 0), (23, 1)]):
-                    mx_pass(bank[:], n, e, g, jh * 256, (jh + 1) * 256, c == 0, c == 3)
-                nc.scalar.activation(out=tl[(m, "z")][:, cols], in_=bank[:], func=ACTF.Sigmoid, bias=bias_s[:, 8 + m:9 + m], scale=-1.0)
-            EE(6, cols)
-            EE(7, cols)
-        for jh in range(2):
-            OT(3, jh)
             OE(3, jh)
-            ST(3, slice(2 * jh, 2 * jh + 2))
+            ST(3, jh)

@@ -61,10 +61,9 @@ def tile_gru_kernel(tc, x, hidden, Wir_w, Wir_b, Whr_w, Whr_b, Wiz_w, Wiz_b, Whz
             w_raw.append(raw.tile([P, 2 * K], BF16, name="w_raw_%d" % n))
 
         def load_act(nm, src):
-            view = src.rearrange("(q j) k -> q (j k)", j=4)
+            view = src.rearrange("(j q) k -> j q k", j=4)
             for j in range(4):
-                cols = slice(j * K, (j + 1) * K)
-                nc.sync.dma_start(out=act_raw[nm][:, cols], in_=view[:, cols])
+                nc.sync.dma_start(out=act_raw[nm][:, j * K:(j + 1) * K], in_=view[j])
 
         def load_w(n, parts):
             w, s = UNITS[n]
@@ -82,7 +81,13 @@ def tile_gru_kernel(tc, x, hidden, Wir_w, Wir_b, Whr_w, Whr_b, Wiz_w, Wiz_b, Whz
         load_w(3, 1)
         for v in range(6):
             nc.sync.dma_start(out=b_raw[4 * v:4 * v + 4, :], in_=biases[v].rearrange("(s c) -> s c", s=4))
-        for n in range(4, 24):
+        for n in range(4, 12):
+            load_w(n, 1)
+        h_v = raw.tile([P, 16, 64], BF16, name="h_v")
+        h_view = hidden.rearrange("(J c) k -> c J k", c=32)
+        for a in range(4):
+            nc.sync.dma_start(out=h_v[32 * a:32 * a + 32], in_=h_view[:, :, a * 64:a * 64 + 64])
+        for n in range(12, 24):
             load_w(n, 1)
 
         banks = {}
@@ -206,7 +211,7 @@ def tile_gru_kernel(tc, x, hidden, Wir_w, Wir_b, Whr_w, Whr_b, Wiz_w, Wiz_b, Whz
             s, e = divmod(m, 2)
             g, u = divmod(s, 2)
             h_t = a_grp["h"][:].rearrange("p (j g q t) -> p j g q t", j=4, g=2, t=4)[:, :, g, :, 2 * u + e]
-            tl[(m, "o")] = eph.tile([P, B], F32, name="o")
+            tl[(m, "o")] = eph.tile([P, B], F32, name="o", align_bytes=64)
             nc.vector.tensor_tensor(out=tl[(m, "o")][:].rearrange("p (j q) -> p j q", j=4), in0=h_t,
                                     in1=tl[(m, "n")][:].rearrange("p (j q) -> p j q", j=4), op=ALU.subtract)
 
@@ -215,7 +220,21 @@ def tile_gru_kernel(tc, x, hidden, Wir_w, Wir_b, Whr_w, Whr_b, Wiz_w, Wiz_b, Whz
             nc.vector.tensor_tensor(out=tl[(m, "o")][:, cols], in0=tl[(m, "z")][:, cols], in1=tl[(m, "o")][:, cols], op=ALU.mult)
 
         o_sb = {}
-        out_v = out.rearrange("(q j) o -> q j o", j=4)
+        out_v = out.rearrange("(j q) o -> q j o", j=4)
+        out_c = out.rearrange("(J c) o -> c J o", c=32)
+        vt = const.tile([P, 2, B], F32, name="vt", align_bytes=64)
+
+        def VT(m):
+            nc.vector.transpose(vt[:, m, :], tl[(m, "o")][:])
+
+        def VO():
+            o_sb[0] = osb.tile([P, 4, 256], F32, name="o_sb")
+            nc.vector.tensor_tensor(out=o_sb[0].rearrange("p j (K i e) -> p (j K) i e", K=4, e=2),
+                                    in0=h_v.rearrange("p J (i e) -> p J i e", e=2),
+                                    in1=vt.rearrange("p e (J i) -> p J i e", i=32), op=ALU.subtract)
+            for a in range(4):
+                nc.sync.dma_start(out=out_c[:, :, a * 64:a * 64 + 64],
+                                  in_=o_sb[0].rearrange("p j (K f) -> p (j K) f", f=64)[32 * a:32 * a + 32])
 
         def OT(s, jh):
             bank = pt.tile([P, 4, P], F32, name="tb", tag="tb")
@@ -246,8 +265,7 @@ def tile_gru_kernel(tc, x, hidden, Wir_w, Wir_b, Whr_w, Whr_b, Wiz_w, Wiz_b, Whz
         for j in range(4):
             AT("x", j)
             AE("x", j, "s")
-            if j == 3:
-                dummies(2)
+            dummies(2 if j == 3 else 1)
             AQ("x", j)
         tr_ev(0, 0, "s")
         tr_ev(0, 1, "v")
@@ -263,6 +281,7 @@ def tile_gru_kernel(tc, x, hidden, Wir_w, Wir_b, Whr_w, Whr_b, Wiz_w, Wiz_b, Whz
         for j in range(1, 4):
             AT("h", j)
             AE("h", j, "vs"[j % 2])
+        dummies(1)
         AQ("h", 1)
         tr_ev(2, 0, "v")
         AQ("h", 2)
@@ -273,8 +292,8 @@ def tile_gru_kernel(tc, x, hidden, Wir_w, Wir_b, Whr_w, Whr_b, Wiz_w, Wiz_b, Whz
         tr_ev(3, 0, "s")
         tr_ev(3, 1, "s")
         BIAS_T()
-        QU(3)
         BIAS_V()
+        QU(3)
         MX(2)
         SR(0)
         SR(1)
@@ -325,11 +344,10 @@ def tile_gru_kernel(tc, x, hidden, Wir_w, Wir_b, Whr_w, Whr_b, Wiz_w, Wiz_b, Whz
             SR(b)
             tr_ev(n + 4, 1)
             tr_ev(n + 5, 0)
-            tr_ev(n + 5, 1, "v")
+            tr_ev(n + 5, 1)
             if s == 1:
-                OT(0, 0)
-                OE(0, 0)
-                ST(0, 0)
+                VT(0)
+                VT(1)
             n += 2
             MX(n)
             MX(n + 1)
@@ -346,9 +364,7 @@ def tile_gru_kernel(tc, x, hidden, Wir_w, Wir_b, Whr_w, Whr_b, Wiz_w, Wiz_b, Whz
             tr_ev(n + 5, 0)
             tr_ev(n + 5, 1)
             if s == 1:
-                OT(0, 1)
-                OE(0, 1)
-                ST(0, 1)
+                VO()
 
         MX(18)
         MX(19)
@@ -357,24 +373,25 @@ def tile_gru_kernel(tc, x, hidden, Wir_w, Wir_b, Whr_w, Whr_b, Wiz_w, Wiz_b, Whz
         DD(7)
         QU(21)
         SZ(2)
-        tr_ev(22, 0)
-        EE(2)
         SZ(3)
+        tr_ev(22, 0)
         tr_ev(22, 1)
-        tr_ev(23, 0)
-        tr_ev(23, 1, "v")
+        EE(2)
         EE(3)
-        QU(22)
+        tr_ev(23, 0)
+        tr_ev(23, 1)
         MX(20)
-        MX(21)
-        QU(23)
+        QU(22)
         OT(1, 0)
         OT(1, 1)
+        MX(21)
+        OE(1, 0)
+        ST(1, 0)
+        QU(23)
+        OE(1, 1)
+        ST(1, 1)
         SZ(4)
         SZ(5)
-        for jh in range(2):
-            OE(1, jh)
-            ST(1, jh)
         EE(4)
         EE(5)
         MX(22, (0,))

@@ -244,17 +244,17 @@ def tile_gru_kernel(tc, x, hidden, Wir_w, Wir_b, Whr_w, Whr_b, Wiz_w, Wiz_b, Whz
                     nc.tensor.transpose(bank[:, 2 * jj + e, :], tl[(2 * s + e, "o")][:, j * P:(j + 1) * P], ident[:])
             banks[("o", s, jh)] = bank
 
-        def OE(s, jh):
+        def OE(s, jh, j0=0, j1=2):
             if jh == 0:
                 o_sb[s] = osb.tile([P, 4, 256], F32, name="o_sb")
-            js = slice(2 * jh, 2 * jh + 2)
+            js = slice(2 * jh + j0, 2 * jh + j1)
             h_t = act_raw["h"][:].rearrange("q (j k) -> q j k", j=4)[:, js, s * 256:(s + 1) * 256]
             nc.vector.tensor_tensor(out=o_sb[s][:, js, :].rearrange("q j (p e) -> q j p e", e=2),
                                     in0=h_t.rearrange("q j (p e) -> q j p e", e=2),
-                                    in1=banks[("o", s, jh)].rearrange("q (j e) p -> q j p e", e=2), op=ALU.subtract)
+                                    in1=banks[("o", s, jh)][:, 2 * j0:2 * j1, :].rearrange("q (j e) p -> q j p e", e=2), op=ALU.subtract)
 
-        def ST(s, jh):
-            js = slice(2 * jh, 2 * jh + 2)
+        def ST(s, jh, j0=0, j1=2):
+            js = slice(2 * jh + j0, 2 * jh + j1)
             nc.sync.dma_start(out=out_v[:, js, s * 256:(s + 1) * 256], in_=o_sb[s][:, js, :])
 
         def tr_ev(n, e, eng="s"):
@@ -413,6 +413,8 @@ def tile_gru_kernel(tc, x, hidden, Wir_w, Wir_b, Whr_w, Whr_b, Wiz_w, Wiz_b, Whz
             ST(2, jh)
         EE(7, 256, 512)
         OT(3, 1)
-        for jh in range(2):
-            OE(3, jh)
-            ST(3, jh)
+        OE(3, 0)
+        ST(3, 0)
+        for j in range(2):
+            OE(3, 1, j, j + 1)
+            ST(3, 1, j, j + 1)

@@ -20,9 +20,9 @@ FLOPS = 2 * B * K * H * 6
 IR, HR, HN, IN, IZ, HZ = 0, 1, 2, 3, 4, 5
 SRC = ["x", "h", "h", "x", "x", "h"]
 GATE = ["r", "r", "hn", "in", "z", "z"]
-UNITS = ([(w, 0) for w in (IR, IN, HR, HN, IZ, HZ)]
-         + [(w, s) for s in range(1, 4) for w in (IR, HR, HN, IN)]
-         + [(w, s) for s in range(1, 4) for w in (IZ, HZ)])
+UNITS = ([(w, s) for s in range(3) for w in ((IR, IN, HR, HN, IZ, HZ) if s == 0 else (IR, HR, HN, IN))] + [(w, 1) for w in (IZ, HZ)]
+         + [(w, 3) for w in (IR, HR, HN, IN)] + [(w, s) for s in (2, 3) for w in (IZ, HZ)])
+PAIR = {"r": "abaa", "in": "bbaa", "hn": "aabb", "z": "abba"}
 
 
 def tile_gru_kernel(tc, x, hidden, Wir_w, Wir_b, Whr_w, Whr_b, Wiz_w, Wiz_b, Whz_w, Whz_b,
@@ -83,10 +83,12 @@ def tile_gru_kernel(tc, x, hidden, Wir_w, Wir_b, Whr_w, Whr_b, Wiz_w, Wiz_b, Whz
             nc.sync.dma_start(out=b_raw[4 * v:4 * v + 4, :], in_=biases[v].rearrange("(s c) -> s c", s=4))
         for n in range(4, 12):
             load_w(n, 1)
-        h_v = raw.tile([P, 16, 64], BF16, name="h_v")
+        h_v = raw.tile([P, 2, 16, 64], BF16, name="h_v")
         h_view = hidden.rearrange("(J c) k -> c J k", c=32)
-        for a in range(4):
-            nc.sync.dma_start(out=h_v[32 * a:32 * a + 32], in_=h_view[:, :, a * 64:a * 64 + 64])
+        for s in range(2):
+            for a in range(4):
+                ch = s * 256 + a * 64
+                nc.sync.dma_start(out=h_v[32 * a:32 * a + 32, s], in_=h_view[:, :, ch:ch + 64])
         for n in range(12, 24):
             load_w(n, 1)
 
@@ -162,11 +164,6 @@ def tile_gru_kernel(tc, x, hidden, Wir_w, Wir_b, Whr_w, Whr_b, Wiz_w, Wiz_b, Whz
         acc = {}
         passes = {}
 
-        def pair_of(gate, s):
-            if s == 0:
-                return "b" if gate == "in" else "a"
-            return "ab"[s % 2] if gate in ("r", "in") else "ba"[s % 2]
-
         def MX(n, es=(0, 1), c0=0, c1=B):
             w, s = UNITS[n]
             nm, gate = SRC[w], GATE[w]
@@ -174,7 +171,7 @@ def tile_gru_kernel(tc, x, hidden, Wir_w, Wir_b, Whr_w, Whr_b, Wiz_w, Wiz_b, Whz
             for e in es:
                 key = (2 * s + e, gate, c0)
                 if key not in acc:
-                    acc[key] = pg.tile([P, c1 - c0], F32, name="acc", tag="acc_%s%d" % (pair_of(gate, s if c0 == 0 else s - 1), e))
+                    acc[key] = pg.tile([P, c1 - c0], F32, name="acc", tag="acc_%s%d" % (PAIR[gate][s if c0 == 0 else s - 1], e))
                     passes[key] = 0
                 for g in range(2):
                     wc = slice(e * 256 + g * P, e * 256 + (g + 1) * P)
@@ -225,16 +222,19 @@ def tile_gru_kernel(tc, x, hidden, Wir_w, Wir_b, Whr_w, Whr_b, Wiz_w, Wiz_b, Whz
         vt = const.tile([P, 2, B], F32, name="vt", align_bytes=64)
 
         def VT(m):
-            nc.vector.transpose(vt[:, m, :], tl[(m, "o")][:])
+            nc.vector.transpose(vt[:, m % 2, :], tl[(m, "o")][:])
 
-        def VO():
-            o_sb[0] = osb.tile([P, 4, 256], F32, name="o_sb")
-            nc.vector.tensor_tensor(out=o_sb[0].rearrange("p j (K i e) -> p (j K) i e", K=4, e=2),
-                                    in0=h_v.rearrange("p J (i e) -> p J i e", e=2),
+        def VO(s):
+            o_sb[s] = osb.tile([P, 4, 256], F32, name="o_sb")
+            nc.vector.tensor_tensor(out=o_sb[s].rearrange("p j (K i e) -> p (j K) i e", K=4, e=2),
+                                    in0=h_v[:, s].rearrange("p J (i e) -> p J i e", e=2),
                                     in1=vt.rearrange("p e (J i) -> p J i e", i=32), op=ALU.subtract)
+
+        def VS(s):
             for a in range(4):
-                nc.sync.dma_start(out=out_c[:, :, a * 64:a * 64 + 64],
-                                  in_=o_sb[0].rearrange("p j (K f) -> p (j K) f", f=64)[32 * a:32 * a + 32])
+                ch = s * 256 + a * 64
+                nc.sync.dma_start(out=out_c[:, :, ch:ch + 64],
+                                  in_=o_sb[s].rearrange("p j (K f) -> p (j K) f", f=64)[32 * a:32 * a + 32])
 
         def OT(s, jh):
             bank = pt.tile([P, 4, P], F32, name="tb", tag="tb")
@@ -328,68 +328,103 @@ def tile_gru_kernel(tc, x, hidden, Wir_w, Wir_b, Whr_w, Whr_b, Wiz_w, Wiz_b, Whz
         EE(0)
         EE(1)
 
-        for s in range(1, 4):
-            a, b = 2 * s, 2 * s + 1
-            n = 4 * s + 2
+        def r_step(n, s, t):
             MX(n)
             MX(n + 1)
-            if s > 1:
-                DD(a - 2)
-            QU(n + 2)
-            if s > 1:
-                DD(b - 2)
-            QU(n + 3)
-            SR(a)
-            tr_ev(n + 4, 0)
-            SR(b)
-            tr_ev(n + 4, 1)
-            tr_ev(n + 5, 0)
-            tr_ev(n + 5, 1)
-            if s == 1:
-                VT(0)
-                VT(1)
-            n += 2
+            QU(t - 2)
+            QU(t - 1)
+            SR(2 * s)
+            tr_ev(t, 0)
+            SR(2 * s + 1)
+            tr_ev(t, 1)
+            tr_ev(t + 1, 0)
+            tr_ev(t + 1, 1)
+
+        def n_step(n, s, t):
+            a, b = 2 * s, 2 * s + 1
             MX(n)
             MX(n + 1)
             TT(a)
             TT(b)
-            QU(n + 2)
+            QU(t - 2)
             UU(a)
-            QU(n + 3)
+            QU(t - 1)
             UU(b)
-            tr_ev(n + 4, 0)
+            tr_ev(t, 0)
             TH(a)
-            tr_ev(n + 4, 1)
+            tr_ev(t, 1)
             TH(b)
-            tr_ev(n + 5, 0)
-            tr_ev(n + 5, 1)
-            if s == 1:
-                VO()
+            tr_ev(t + 1, 0)
+            tr_ev(t + 1, 1)
 
-        MX(18)
-        MX(19)
-        DD(6)
-        QU(20)
-        DD(7)
-        QU(21)
+        r_step(6, 1, 10)
+        VT(0)
+        VT(1)
+        n_step(8, 1, 12)
+        VO(0)
+        VS(0)
+        MX(10)
+        MX(11)
+        DD(2)
+        QU(12)
+        DD(3)
+        QU(13)
+        SR(4)
+        tr_ev(14, 0)
+        SR(5)
+        tr_ev(14, 1)
+        tr_ev(15, 0)
+        tr_ev(15, 1)
+        n_step(12, 2, 16)
+        MX(14)
+        MX(15)
+        DD(4)
+        QU(16)
+        DD(5)
+        QU(17)
         SZ(2)
         SZ(3)
-        tr_ev(22, 0)
-        tr_ev(22, 1)
+        tr_ev(18, 0)
+        tr_ev(18, 1)
+        tr_ev(19, 0)
+        tr_ev(19, 1)
         EE(2)
         EE(3)
+        MX(16)
+        MX(17)
+        VT(2)
+        QU(18)
+        VT(3)
+        QU(19)
+        VO(1)
+        VS(1)
+        SR(6)
+        tr_ev(20, 0)
+        SR(7)
+        tr_ev(20, 1)
+        tr_ev(21, 0)
+        tr_ev(21, 1)
+        MX(18)
+        MX(19)
+        TT(6)
+        TT(7)
+        QU(20)
+        UU(6)
+        QU(21)
+        UU(7)
+        tr_ev(22, 0)
+        tr_ev(22, 1)
         tr_ev(23, 0)
         tr_ev(23, 1)
+        TH(6)
+        TH(7)
+
         MX(20)
         QU(22)
-        OT(1, 0)
-        OT(1, 1)
         MX(21)
-        OE(1, 0)
-        ST(1, 0)
         QU(23)
-        OE(1, 1)
-        ST(1, 1)
+        DD(6)
+        DD(7)
         SZ(4)
         SZ(5)
         EE(4)
@@ -397,22 +432,19 @@ def tile_gru_kernel(tc, x, hidden, Wir_w, Wir_b, Whr_w, Whr_b, Wiz_w, Wiz_b, Whz
         MX(22, (0,))
         MX(23, (0,))
         SZ(6)
-        MX(22, (1,), 0, 256)
-        MX(23, (1,), 0, 256)
+        for c0 in (0, 256):
+            MX(22, (1,), c0, c0 + 256)
+            MX(23, (1,), c0, c0 + 256)
+            SZ(7, c0, c0 + 256)
         OT(2, 0)
         OT(2, 1)
-        MX(22, (1,), 256, 512)
-        MX(23, (1,), 256, 512)
-        SZ(7, 0, 256)
-        SZ(7, 256, 512)
         EE(6)
-        EE(7, 0, 256)
-        OT(3, 0)
+        for jh in range(2):
+            EE(7, jh * 256, jh * 256 + 256)
+            OT(3, jh)
         for jh in range(2):
             OE(2, jh)
             ST(2, jh)
-        EE(7, 256, 512)
-        OT(3, 1)
         OE(3, 0)
         ST(3, 0)
         for j in range(2):

from contextlib import ExitStack

import concourse.masks as masks
import concourse.mybir as mybir

F32 = mybir.dt.float32
BF16 = mybir.dt.bfloat16
U32 = mybir.dt.uint32
U8 = mybir.dt.uint8
FP8X4 = mybir.dt.float8_e4m3fn_x4
ALU = mybir.AluOpType
ACTF = mybir.ActivationFunctionType

P = 128
B = 512
K = 1024
H = 1024
FLOPS = 2 * B * K * H * 6

IR, HR, HN, IN, IZ, HZ = 0, 1, 2, 3, 4, 5
SRC = ["x", "h", "h", "x", "x", "h"]
GATE = ["r", "r", "hn", "in", "z", "z"]
UNITS = ([(w, s) for s in range(3) for w in ((IR, IN, HR, HN, IZ, HZ) if s == 0 else (IR, HR, HN, IN))] + [(w, 1) for w in (IZ, HZ)]
         + [(w, 3) for w in (IR, HR, HN, IN)] + [(w, s) for s in (2, 3) for w in (IZ, HZ)])
PAIR = {"r": "abaa", "in": "bbaa", "hn": "aabb", "z": "abba"}


def tile_gru_kernel(tc, x, hidden, Wir_w, Wir_b, Whr_w, Whr_b, Wiz_w, Wiz_b, Whz_w, Whz_b,
                               Win_w, Win_b, Whn_w, Whn_b, out):
    nc = tc.nc
    weights = [Wir_w, Whr_w, Whn_w, Win_w, Wiz_w, Whz_w]
    biases = [Wir_b, Whr_b, Wiz_b, Whz_b, Win_b, Whn_b]
    with ExitStack() as ctx:
        ctx.enter_context(tc.manual_schedule())
        const = ctx.enter_context(tc.tile_pool(name="const", bufs=1))
        raw = ctx.enter_context(tc.tile_pool(name="raw", bufs=1))
        keep = ctx.enter_context(tc.tile_pool(name="keep", bufs=1))
        grp = ctx.enter_context(tc.tile_pool(name="grp", bufs=4))
        cod = ctx.enter_context(tc.tile_pool(name="cod", bufs=5))
        ep = ctx.enter_context(tc.tile_pool(name="ep", bufs=4))
        eph = ctx.enter_context(tc.tile_pool(name="eph", bufs=6))
        osb = ctx.enter_context(tc.tile_pool(name="osb", bufs=2))
        pt = ctx.enter_context(tc.psum_pool(name="pt", bufs=4))
        pg = ctx.enter_context(tc.psum_pool(name="pg", bufs=1))

        idle = const.tile([P, 512], BF16, name="idle")
        nc.vector.memset(idle[:], 0.0)
        b_raw = const.tile([P, 2 * P], BF16, name="b_raw")
        nc.vector.memset(b_raw[:], 0.0)
        ident = const.tile([P, P], F32, name="ident")
        masks.make_identity(nc, ident[:])
        warm = const.tile([P, 1], F32, name="warm")
        nc.vector.memset(warm[:], 0.0)
        nc.scalar.activation(out=warm[:], in_=warm[:], func=ACTF.Sigmoid)

        act_raw = {}
        for nm in ("x", "h"):
            act_raw[nm] = raw.tile([P, 4 * K], BF16, name="raw_" + nm)
        w_raw = []
        for n in range(24):
            w_raw.append(raw.tile([P, 2 * K], BF16, name="w_raw_%d" % n))

        def load_act(nm, src):
            view = src.rearrange("(j q) k -> j q k", j=4)
            for j in range(4):
                nc.sync.dma_start(out=act_raw[nm][:, j * K:(j + 1) * K], in_=view[j])

        def load_w(n, parts):
            w, s = UNITS[n]
            view = weights[w].rearrange("(s q e) k -> s q (e k)", s=4, e=2)[s]
            width = 2 * K // parts
            for c in range(parts):
                cols = slice(c * width, (c + 1) * width)
                nc.sync.dma_start(out=w_raw[n][:, cols], in_=view[:, cols])

        load_act("x", x)
        load_w(0, 2)
        load_w(1, 2)
        load_act("h", hidden)
        load_w(2, 1)
        load_w(3, 1)
        for v in range(6):
            nc.sync.dma_start(out=b_raw[4 * v:4 * v + 4, :], in_=biases[v].rearrange("(s c) -> s c", s=4))
        for n in range(4, 12):
            load_w(n, 1)
        h_v = raw.tile([P, 2, 16, 64], BF16, name="h_v")
        h_view = hidden.rearrange("(J c) k -> c J k", c=32)
        for s in range(2):
            for a in range(4):
                ch = s * 256 + a * 64
                nc.sync.dma_start(out=h_v[32 * a:32 * a + 32, s], in_=h_view[:, :, ch:ch + 64])
        for n in range(12, 24):
            load_w(n, 1)

        banks = {}

        def transposes(key, words):
            bank = pt.tile([P, 4, P], F32, name="tb", tag="tb")
            for c in range(4):
                nc.tensor.transpose(bank[:, c, :], words[:, c * P:(c + 1) * P], ident[:])
            banks[key] = bank

        def dummies(n):
            bank = pg.tile([P, B], F32, name="acc", tag="acc_b1")
            for c in range(n):
                nc.tensor.matmul(bank[:], idle[:, 0:P], idle[:], start=True, stop=True)

        def copy_out(eng, dst, src):
            if eng == "s":
                nc.scalar.copy(out=dst, in_=src)
            else:
                nc.vector.tensor_copy(out=dst, in_=src)

        a_grp, a_cod, a_scl = {}, {}, {}
        for nm in ("x", "h"):
            a_grp[nm] = keep.tile([P, 4 * K], BF16, name="grp_" + nm, align_bytes=64)
            a_cod[nm] = keep.tile([P, K], U32, name="cod_" + nm, align_bytes=64)
            a_scl[nm] = keep.tile([P, K], U8, name="scl_" + nm, align_bytes=64)

        def AT(nm, j):
            transposes((nm, j), act_raw[nm][:].bitcast(F32)[:, j * 512:(j + 1) * 512])

        def AE(nm, j, eng):
            dst = a_grp[nm][:].bitcast(F32)[:, j * 512:(j + 1) * 512].rearrange("p (g q u) -> p g q u", g=2, u=2)
            copy_out(eng, dst, banks[(nm, j)].rearrange("p (g u) q -> p g q u", g=2))

        def AQ(nm, j):
            for g in range(2):
                cols = slice(g * B + j * P, g * B + (j + 1) * P)
                nc.vector.quantize_mx(out=a_cod[nm][:, cols].bitcast(FP8X4), scales=a_scl[nm][:, cols],
                                      in_=a_grp[nm][:, (2 * j + g) * 512:(2 * j + g + 1) * 512])

        bias_f = const.tile([P, 64], F32, name="bias_f")
        bias_s = const.tile([P, 16], F32, name="bias_s")
        bias_w = const.tile([P, 32], F32, name="bias_w")

        def BIAS_T():
            bank = pt.tile([P, 4, P], F32, name="tb", tag="tb")
            nc.tensor.transpose(bank[:, 0, :], b_raw[:].bitcast(F32), ident[:])
            nc.vector.tensor_copy(out=bias_w[:], in_=bank[:, 0, 0:32])

        def BIAS_V():
            nc.vector.tensor_copy(out=bias_f[:], in_=bias_w[:].bitcast(BF16))
            nc.vector.tensor_tensor(out=bias_s[:, 0:8], in0=bias_f[:, 0:8], in1=bias_f[:, 8:16], op=ALU.add)
            nc.vector.scalar_tensor_tensor(out=bias_s[:, 8:16], in0=bias_f[:, 16:24], scalar=-1.0, in1=bias_f[:, 24:32],
                                           op0=ALU.mult, op1=ALU.subtract)

        w_grp, w_cod, w_scl = {}, {}, {}

        def TR(n, e):
            transposes((n, e), w_raw[n][:].bitcast(F32)[:, e * 512:(e + 1) * 512])

        def EV(n, e, eng="s"):
            if n not in w_grp:
                w_grp[n] = grp.tile([P, 2 * K], BF16, name="w_grp", tag="w_grp", align_bytes=64)
            dst = w_grp[n][:].bitcast(F32)[:, e * 512:(e + 1) * 512].rearrange("p (g q u) -> p g q u", g=2, u=2)
            copy_out(eng, dst, banks[(n, e)].rearrange("p (g u) q -> p g q u", g=2))

        def QU(n):
            w_cod[n] = cod.tile([P, 512], U32, name="w_cod", tag="w_cod", align_bytes=64)
            w_scl[n] = cod.tile([P, 512], U8, name="w_scl", tag="w_scl", align_bytes=64)
            nc.vector.quantize_mx(out=w_cod[n][:].bitcast(FP8X4), scales=w_scl[n][:], in_=w_grp[n][:])

        acc = {}
        passes = {}

        def MX(n, es=(0, 1), c0=0, c1=B):
            w, s = UNITS[n]
            nm, gate = SRC[w], GATE[w]
            total = 2 if gate in ("hn", "in") else 4
            for e in es:
                key = (2 * s + e, gate, c0)
                if key not in acc:
                    acc[key] = pg.tile([P, c1 - c0], F32, name="acc", tag="acc_%s%d" % (PAIR[gate][s if c0 == 0 else s - 1], e))
                    passes[key] = 0
                for g in range(2):
                    wc = slice(e * 256 + g * P, e * 256 + (g + 1) * P)
                    ac = slice(g * B + c0, g * B + c1)
                    passes[key] += 1
                    nc.tensor.matmul_mx(out=acc[key][:], lhsT=w_cod[n][:, wc].bitcast(FP8X4), lhsT_scale=w_scl[n][:, wc],
                                        rhs=a_cod[nm][:, ac].bitcast(FP8X4), rhs_scale=a_scl[nm][:, ac],
                                        start=passes[key] == 1, stop=passes[key] == total)

        tl = {}

        def SR(m):
            tl[(m, "r")] = ep.tile([P, B], F32, name="r")
            nc.scalar.activation(out=tl[(m, "r")][:], in_=acc[(m, "r", 0)][:], func=ACTF.Sigmoid, bias=bias_s[:, m:m + 1], scale=1.0)

        def SZ(m, c0=0, c1=B):
            if (m, "z") not in tl:
                tl[(m, "z")] = ep.tile([P, B], F32, name="z")
            nc.scalar.activation(out=tl[(m, "z")][:, c0:c1], in_=acc[(m, "z", c0)][:], func=ACTF.Sigmoid, bias=bias_s[:, 8 + m:9 + m], scale=-1.0)

        def TT(m):
            tl[(m, "t")] = ep.tile([P, B], F32, name="t")
            nc.vector.scalar_tensor_tensor(out=tl[(m, "t")][:], in0=acc[(m, "hn", 0)][:], scalar=bias_f[:, 40 + m:41 + m],
                                           in1=tl[(m, "r")][:], op0=ALU.add, op1=ALU.mult)

        def UU(m):
            nc.vector.tensor_tensor(out=tl[(m, "t")][:], in0=acc[(m, "in", 0)][:], in1=tl[(m, "t")][:], op=ALU.add)

        def TH(m):
            tl[(m, "n")] = ep.tile([P, B], F32, name="n")
            nc.scalar.activation(out=tl[(m, "n")][:], in_=tl[(m, "t")][:], func=ACTF.Tanh, bias=bias_f[:, 32 + m:33 + m], scale=1.0)

        def DD(m):
            s, e = divmod(m, 2)
            g, u = divmod(s, 2)
            h_t = a_grp["h"][:].rearrange("p (j g q t) -> p j g q t", j=4, g=2, t=4)[:, :, g, :, 2 * u + e]
            tl[(m, "o")] = eph.tile([P, B], F32, name="o", align_bytes=64)
            nc.vector.tensor_tensor(out=tl[(m, "o")][:].rearrange("p (j q) -> p j q", j=4), in0=h_t,
                                    in1=tl[(m, "n")][:].rearrange("p (j q) -> p j q", j=4), op=ALU.subtract)

        def EE(m, c0=0, c1=B):
            cols = slice(c0, c1)
            nc.vector.tensor_tensor(out=tl[(m, "o")][:, cols], in0=tl[(m, "z")][:, cols], in1=tl[(m, "o")][:, cols], op=ALU.mult)

        o_sb = {}
        out_v = out.rearrange("(j q) o -> q j o", j=4)
        out_c = out.rearrange("(J c) o -> c J o", c=32)
        vt = const.tile([P, 2, B], F32, name="vt", align_bytes=64)

        def VT(m):
            nc.vector.transpose(vt[:, m % 2, :], tl[(m, "o")][:])

        def VO(s):
            o_sb[s] = osb.tile([P, 4, 256], F32, name="o_sb")
            nc.vector.tensor_tensor(out=o_sb[s].rearrange("p j (K i e) -> p (j K) i e", K=4, e=2),
                                    in0=h_v[:, s].rearrange("p J (i e) -> p J i e", e=2),
                                    in1=vt.rearrange("p e (J i) -> p J i e", i=32), op=ALU.subtract)

        def VS(s):
            for a in range(4):
                ch = s * 256 + a * 64
                nc.sync.dma_start(out=out_c[:, :, ch:ch + 64],
                                  in_=o_sb[s].rearrange("p j (K f) -> p (j K) f", f=64)[32 * a:32 * a + 32])

        def OT(s, jh):
            bank = pt.tile([P, 4, P], F32, name="tb", tag="tb")
            for jj in range(2):
                for e in range(2):
                    j = 2 * jh + jj
                    nc.tensor.transpose(bank[:, 2 * jj + e, :], tl[(2 * s + e, "o")][:, j * P:(j + 1) * P], ident[:])
            banks[("o", s, jh)] = bank

        def OE(s, jh, j0=0, j1=2):
            if jh == 0:
                o_sb[s] = osb.tile([P, 4, 256], F32, name="o_sb")
            js = slice(2 * jh + j0, 2 * jh + j1)
            h_t = act_raw["h"][:].rearrange("q (j k) -> q j k", j=4)[:, js, s * 256:(s + 1) * 256]
            nc.vector.tensor_tensor(out=o_sb[s][:, js, :].rearrange("q j (p e) -> q j p e", e=2),
                                    in0=h_t.rearrange("q j (p e) -> q j p e", e=2),
                                    in1=banks[("o", s, jh)][:, 2 * j0:2 * j1, :].rearrange("q (j e) p -> q j p e", e=2), op=ALU.subtract)

        def ST(s, jh, j0=0, j1=2):
            js = slice(2 * jh + j0, 2 * jh + j1)
            nc.sync.dma_start(out=out_v[:, js, s * 256:(s + 1) * 256], in_=o_sb[s][:, js, :])

        def tr_ev(n, e, eng="s"):
            TR(n, e)
            EV(n, e, eng)

        dummies(5)
        for j in range(4):
            AT("x", j)
            AE("x", j, "s")
            dummies(2 if j == 3 else 1)
            AQ("x", j)
        tr_ev(0, 0, "s")
        tr_ev(0, 1, "v")
        dummies(2)
        QU(0)
        tr_ev(1, 0, "s")
        tr_ev(1, 1, "s")
        AT("h", 0)
        AE("h", 0, "v")
        MX(0)
        QU(1)
        AQ("h", 0)
        for j in range(1, 4):
            AT("h", j)
            AE("h", j, "vs"[j % 2])
        dummies(1)
        AQ("h", 1)
        tr_ev(2, 0, "v")
        AQ("h", 2)
        tr_ev(2, 1, "s")
        AQ("h", 3)
        QU(2)
        MX(1)
        tr_ev(3, 0, "s")
        tr_ev(3, 1, "s")
        BIAS_T()
        BIAS_V()
        QU(3)
        MX(2)
        SR(0)
        SR(1)
        tr_ev(4, 0, "v")
        tr_ev(4, 1)
        tr_ev(5, 0)
        tr_ev(5, 1)
        MX(3)
        QU(4)
        TT(0)
        TT(1)
        QU(5)
        UU(0)
        UU(1)
        for n in (6, 7):
            tr_ev(n, 0)
            tr_ev(n, 1)
        TH(0)
        TH(1)
        MX(4)
        MX(5)
        DD(0)
        QU(6)
        DD(1)
        QU(7)
        SZ(0)
        tr_ev(8, 0)
        SZ(1)
        tr_ev(8, 1)
        tr_ev(9, 0)
        tr_ev(9, 1)
        EE(0)
        EE(1)

        def r_step(n, s, t):
            MX(n)
            MX(n + 1)
            QU(t - 2)
            QU(t - 1)
            SR(2 * s)
            tr_ev(t, 0)
            SR(2 * s + 1)
            tr_ev(t, 1)
            tr_ev(t + 1, 0)
            tr_ev(t + 1, 1)

        def n_step(n, s, t):
            a, b = 2 * s, 2 * s + 1
            MX(n)
            MX(n + 1)
            TT(a)
            TT(b)
            QU(t - 2)
            UU(a)
            QU(t - 1)
            UU(b)
            tr_ev(t, 0)
            TH(a)
            tr_ev(t, 1)
            TH(b)
            tr_ev(t + 1, 0)
            tr_ev(t + 1, 1)

        r_step(6, 1, 10)
        VT(0)
        VT(1)
        n_step(8, 1, 12)
        VO(0)
        VS(0)
        MX(10)
        MX(11)
        DD(2)
        QU(12)
        DD(3)
        QU(13)
        SR(4)
        tr_ev(14, 0)
        SR(5)
        tr_ev(14, 1)
        tr_ev(15, 0)
        tr_ev(15, 1)
        n_step(12, 2, 16)
        MX(14)
        MX(15)
        DD(4)
        QU(16)
        DD(5)
        QU(17)
        SZ(2)
        SZ(3)
        tr_ev(18, 0)
        tr_ev(18, 1)
        tr_ev(19, 0)
        tr_ev(19, 1)
        EE(2)
        EE(3)
        MX(16)
        MX(17)
        VT(2)
        QU(18)
        VT(3)
        QU(19)
        VO(1)
        VS(1)
        SR(6)
        tr_ev(20, 0)
        SR(7)
        tr_ev(20, 1)
        tr_ev(21, 0)
        tr_ev(21, 1)
        MX(18)
        MX(19)
        TT(6)
        TT(7)
        QU(20)
        UU(6)
        QU(21)
        UU(7)
        tr_ev(22, 0)
        tr_ev(22, 1)
        tr_ev(23, 0)
        tr_ev(23, 1)
        TH(6)
        TH(7)

        MX(20)
        QU(22)
        MX(21)
        QU(23)
        DD(6)
        DD(7)
        SZ(4)
        SZ(5)
        EE(4)
        EE(5)
        MX(22, (0,))
        MX(23, (0,))
        SZ(6)
        for c0 in (0, 256):
            MX(22, (1,), c0, c0 + 256)
            MX(23, (1,), c0, c0 + 256)
            SZ(7, c0, c0 + 256)
        OT(2, 0)
        OT(2, 1)
        EE(6)
        for jh in range(2):
            EE(7, jh * 256, jh * 256 + 256)
            OT(3, jh)
        for jh in range(2):
            OE(2, jh)
            ST(2, jh)
        OE(3, 0)
        ST(3, 0)
        for j in range(2):
            OE(3, 1, j, j + 1)
            ST(3, 1, j, j + 1)
